import numpy as np
import ml_dtypes


def mxq(x, axis, fmt="e4m3"):
    dtype, down = {"e4m3": (ml_dtypes.float8_e4m3fn, 7), "e5m2": (ml_dtypes.float8_e5m2, 14)}[fmt]
    v = np.moveaxis(np.asarray(x, np.float32).astype(ml_dtypes.bfloat16).astype(np.float64), axis, -1)
    blocks = v.reshape(v.shape[:-1] + (-1, 32))
    amax = np.abs(blocks).max(-1, keepdims=True)
    byte = np.maximum(np.where(amax > 0, np.frexp(amax)[1] - 1 + 127, 0) - down, 1)
    scale = np.exp2(byte - 127.0)
    codes = (blocks / scale).astype(np.float32).astype(dtype).astype(np.float64)
    return np.moveaxis((codes * scale).reshape(v.shape), -1, axis)


WIDE = False


def mx_kscale(k):
    if not WIDE:
        return np.ones(k)
    levels = np.array([10, -10, 5, -5, 0])
    if k % 512:
        return np.exp2(np.random.permutation(np.resize(levels, k // 32))).repeat(32)
    a = np.empty((k // 512, 16))
    for p in range(k // 512):
        a[p, :8] = np.random.permutation(np.resize(levels, 8))
        for g in range(8):
            far = levels[np.abs(levels - a[p, g]) >= 10]
            a[p, g + 8] = far[np.random.randint(len(far))]
    return np.exp2(a.ravel()).repeat(32)


BF16 = ml_dtypes.bfloat16


def bf(x):
    return np.asarray(x, np.float32).astype(BF16)


def f64(x):
    return np.asarray(x).astype(np.float64)


B, N, NIN, CTX, H, NOUT = 2, 64, 512, 3, 512, 2
F = NIN * CTX


def shift_down(y, d):
    return np.pad(y[:, :-d, :], ((0, 0), (d, 0), (0, 0)))


def shift_up(y, d):
    return np.pad(y[:, d:, :], ((0, 0), (0, d), (0, 0)))


def context_linear(xq, w, shifts):
    y = xq @ mxq(w[:, :NIN].T, 0, "e4m3")
    c = 1
    for d in range(1, CTX // 2 + 1):
        for shift in shifts:
            y = y + shift(xq @ mxq(w[:, c * NIN:(c + 1) * NIN].T, 0, "e4m3"), d)
            c += 1
    return y


def setup_inputs():
    s, u = mx_kscale(NIN), mx_kscale(H)
    return {"x_l": bf(np.random.standard_normal((B, N, NIN)) * s),
            "W_l": bf(np.random.standard_normal((H, F)) / np.sqrt(F) / np.tile(s, CTX) * u[:, None]),
            "b_l": bf(np.random.standard_normal(H) * 0.3 * u),
            "W_bil": bf(np.random.standard_normal((NOUT, H, H)) * 0.2 / np.sqrt(H) / u[None, :, None])}


def reference(x_l, W_l, b_l, W_bil):
    xq = mxq(f64(x_l), 2, "e4m3")
    hl = np.maximum(context_linear(xq, f64(W_l), (shift_down, shift_up)) + f64(b_l), 0.0)
    wb = f64(W_bil).transpose(1, 0, 2).reshape(H, NOUT * H)
    t = mxq(hl, 2, "e4m3") @ mxq(wb, 0, "e4m3")
    return t.reshape(B, N, NOUT, H)

@@ -1,0 +1,198 @@
+from contextlib import ExitStack
+
+import concourse.mybir as mybir
+from concourse.masks import make_identity
+
+F32 = mybir.dt.float32
+BF16 = mybir.dt.bfloat16
+U32 = mybir.dt.uint32
+U8 = mybir.dt.uint8
+FP8X4 = mybir.dt.float8_e4m3fn_x4
+RELU = mybir.ActivationFunctionType.Relu
+
+P = 128
+PACK = 4
+BATCH = 2
+SEQ = 64
+TOK = BATCH * SEQ
+NIN = 512
+WINDOWS = 3
+H = 512
+H_TILES = H // P
+NOUT = 2
+
+HALVES = 2
+ITEMS = H_TILES * WINDOWS
+ITEMS_PER_BANK = 2
+WL_BANKS = ITEMS // ITEMS_PER_BANK
+WL_CHUNK = ITEMS_PER_BANK * NIN
+
+UNIT = 256
+UNITS = NOUT * H // UNIT
+UNITS_PER_MAP = H // UNIT
+VECTOR_COLS = 160
+
+FLOPS = 2 * TOK * (WINDOWS * NIN) * H + 2 * TOK * H * (NOUT * H)
+
+
+def tile_bilinearpairedlayer_pa_s_kernel(tc, x_l, W_l, b_l, W_bil, out):
+    nc = tc.nc
+    with ExitStack() as ctx:
+        keep = ctx.enter_context(tc.tile_pool(name="keep", bufs=1))
+        psum_one = ctx.enter_context(tc.psum_pool(name="psum_one", bufs=6))
+        psum_two = ctx.enter_context(tc.psum_pool(name="psum_two", bufs=2))
+        ctx.enter_context(tc.manual_schedule())
+
+        x_raw = keep.tile([P, NIN], BF16)
+        nc.sync.dma_start(out=x_raw[:], in_=x_l.rearrange("b i f -> (b i) f"))
+        bias = keep.tile([P, PACK], BF16)
+        nc.scalar.dma_start(out=bias[:], in_=b_l.rearrange("(p t) -> p t", t=PACK))
+        wl_rows = W_l.rearrange("(p t) f -> p (t f)", t=PACK)
+        wl_raw = []
+        for n in range(WL_BANKS):
+            chunk = keep.tile([P, WL_CHUNK], BF16, name="wl_raw%d" % n)
+            nc.sync.dma_start(out=chunk[:], in_=wl_rows[:, n * WL_CHUNK : (n + 1) * WL_CHUNK])
+            wl_raw.append(chunk)
+        wb_raw = []
+        for k in range(NOUT):
+            chunk = keep.tile([P, PACK, H], BF16, name="wb_raw%d" % k)
+            nc.sync.dma_start(out=chunk[:], in_=W_bil[k].rearrange("(p t) g -> p t g", t=PACK))
+            wb_raw.append(chunk)
+
+        ident = keep.tile([P, P], F32)
+        make_identity(nc, ident[:])
+
+        x_grouped = keep.tile([P, WINDOWS * TOK * PACK], BF16, align_bytes=64)
+        nc.vector.memset(x_grouped[:], 0.0)
+        x_words = x_raw[:].bitcast(F32)
+        xT = psum_one.tile([P, HALVES, TOK], F32, tag="bank")
+        for u in range(HALVES):
+            nc.tensor.transpose(xT[:, u, :], x_words[:, u : HALVES * P : HALVES], ident[:])
+        xT_view = xT[:].rearrange("p u (b i) -> p b i u", b=BATCH)
+        xg_words = x_grouped[:].bitcast(F32).rearrange(
+            "p (c b i u) -> p c b i u", c=WINDOWS, b=BATCH, u=HALVES
+        )
+        nc.vector.tensor_copy(out=xg_words[:, 0], in_=xT_view)
+        nc.vector.tensor_copy(out=xg_words[:, 1, :, 1:SEQ, :], in_=xT_view[:, :, 0 : SEQ - 1, :])
+        nc.vector.tensor_copy(out=xg_words[:, 2, :, 0 : SEQ - 1, :], in_=xT_view[:, :, 1:SEQ, :])
+        x_codes = keep.tile([P, WINDOWS, TOK], U32, align_bytes=64)
+        x_scales = keep.tile([P, WINDOWS, TOK], U8, align_bytes=64)
+        for c in range(WINDOWS):
+            nc.vector.quantize_mx(
+                out=x_codes[:, c, :].bitcast(FP8X4),
+                scales=x_scales[:, c, :],
+                in_=x_grouped[:, c * TOK * PACK : (c + 1) * TOK * PACK],
+            )
+
+        wl_grouped = keep.tile([P, ITEMS * P * PACK], BF16, align_bytes=64)
+        wlg_words = wl_grouped[:].bitcast(F32).rearrange("p (a h u) -> p a h u", a=ITEMS, u=HALVES)
+        wl_codes = keep.tile([P, ITEMS * P], U32, align_bytes=64)
+        wl_scales = keep.tile([P, ITEMS * P], U8, align_bytes=64)
+        for n in range(WL_BANKS):
+            wl_words = wl_raw[n][:].bitcast(F32)
+            wT = psum_one.tile([P, ITEMS_PER_BANK * HALVES, P], F32, tag="bank")
+            for j in range(ITEMS_PER_BANK * HALVES):
+                nc.tensor.transpose(wT[:, j, :], wl_words[:, (j // HALVES) * HALVES * P + j % HALVES : (j // HALVES + 1) * HALVES * P : HALVES], ident[:])
+            nc.scalar.copy(
+                out=wlg_words[:, n * ITEMS_PER_BANK : (n + 1) * ITEMS_PER_BANK, :, :],
+                in_=wT[:].rearrange("p (a u) h -> p a h u", u=HALVES),
+            )
+            nc.vector.quantize_mx(
+                out=wl_codes[:, n * ITEMS_PER_BANK * P : (n + 1) * ITEMS_PER_BANK * P].bitcast(FP8X4),
+                scales=wl_scales[:, n * ITEMS_PER_BANK * P : (n + 1) * ITEMS_PER_BANK * P],
+                in_=wl_grouped[:, n * WL_CHUNK : (n + 1) * WL_CHUNK],
+            )
+
+        hlT = keep.tile([P, H_TILES, TOK], BF16)
+
+        def layer1_tile(t):
+            pre = psum_one.tile([P, TOK], F32, tag="bank")
+            for c in range(WINDOWS):
+                a = t * WINDOWS + c
+                nc.tensor.matmul_mx(
+                    out=pre[:],
+                    lhsT=wl_codes[:, a * P : (a + 1) * P].bitcast(FP8X4),
+                    lhsT_scale=wl_scales[:, a * P : (a + 1) * P],
+                    rhs=x_codes[:, c, :].bitcast(FP8X4),
+                    rhs_scale=x_scales[:, c, :],
+                    start=(c == 0),
+                    stop=(c == WINDOWS - 1),
+                )
+            return pre
+
+        def relu_tile(t, pre):
+            nc.scalar.activation(
+                out=hlT[:, t, :], in_=pre[:], func=RELU, bias=bias[:, t : t + 1], scale=1.0
+            )
+
+        wb_grouped = keep.tile([P, UNITS, UNIT, PACK], BF16, align_bytes=64)
+        wb_codes = keep.tile([P, UNITS, UNIT], U32, align_bytes=64)
+        wb_scales = keep.tile([P, UNITS, UNIT], U8, align_bytes=64)
+
+        def regroup_unit(q):
+            raw = wb_raw[q // UNITS_PER_MAP]
+            g0 = (q % UNITS_PER_MAP) * UNIT
+            nc.vector.tensor_copy(
+                out=wb_grouped[:, q, 0:VECTOR_COLS, :].rearrange("p (c i) t -> p c t i", i=4),
+                in_=raw[:, :, g0 : g0 + VECTOR_COLS].rearrange("p t (c i) -> p c t i", i=4),
+            )
+            nc.scalar.copy(
+                out=wb_grouped[:, q, VECTOR_COLS:UNIT, :].rearrange("p (c i) t -> p c t i", i=4),
+                in_=raw[:, :, g0 + VECTOR_COLS : g0 + UNIT].rearrange("p t (c i) -> p c t i", i=4),
+            )
+
+        def quantise_unit(q):
+            nc.vector.quantize_mx(
+                out=wb_codes[:, q, :].bitcast(FP8X4),
+                scales=wb_scales[:, q, :],
+                in_=wb_grouped[:, q, :, :].rearrange("p g t -> p (g t)"),
+            )
+
+        hl_grouped = keep.tile([P, TOK, PACK], BF16, align_bytes=64)
+        hl_codes = keep.tile([P, TOK], U32, align_bytes=64)
+        hl_scales = keep.tile([P, TOK], U8, align_bytes=64)
+
+        def regroup_hl():
+            nc.vector.tensor_copy(out=hl_grouped[:], in_=hlT[:].rearrange("p t r -> p r t"))
+
+        def quantise_hl():
+            nc.vector.quantize_mx(
+                out=hl_codes[:].bitcast(FP8X4),
+                scales=hl_scales[:],
+                in_=hl_grouped[:].rearrange("p r t -> p (r t)"),
+            )
+
+        out_rows = out.rearrange("b i k g -> (b i) (k g)")
+
+        def layer2_unit(q):
+            acc = psum_two.tile([P, UNIT], F32)
+            nc.tensor.matmul_mx(
+                out=acc[:],
+                lhsT=hl_codes[:].bitcast(FP8X4),
+                lhsT_scale=hl_scales[:],
+                rhs=wb_codes[:, q, :].bitcast(FP8X4),
+                rhs_scale=wb_scales[:, q, :],
+                start=True,
+                stop=True,
+            )
+            result = keep.tile([P, UNIT], F32, name="result%d" % q)
+            if q % 2 == 0:
+                nc.scalar.copy(out=result[:], in_=acc[:])
+            else:
+                nc.vector.tensor_copy(out=result[:], in_=acc[:])
+            nc.sync.dma_start(out=out_rows[:, q * UNIT : (q + 1) * UNIT], in_=result[:])
+
+        regroup_unit(0)
+        for t in range(H_TILES):
+            relu_tile(t, layer1_tile(t))
+        regroup_unit(1)
+        regroup_unit(2)
+        quantise_unit(0)
+        regroup_hl()
+        quantise_unit(1)
+        quantise_hl()
+        regroup_unit(3)
+        quantise_unit(2)
+        quantise_unit(3)
+        for q in range(UNITS):
+            layer2_unit(q)

@@ -32,6 +32,9 @@ UNITS = NOUT * H // UNIT
 UNITS_PER_MAP = H // UNIT
 VECTOR_COLS = 160
 
+WARM_COLS = 256
+WARM_PASSES = 2
+
 FLOPS = 2 * TOK * (WINDOWS * NIN) * H + 2 * TOK * H * (NOUT * H)
 
 
@@ -61,6 +64,12 @@ def tile_bilinearpairedlayer_pa_s_kernel(tc, x_l, W_l, b_l, W_bil, out):
 
         ident = keep.tile([P, P], F32)
         make_identity(nc, ident[:])
+
+        zeros = keep.tile([P, WARM_COLS], F32)
+        nc.vector.memset(zeros[:], 0.0)
+        for i in range(WARM_PASSES):
+            unread = psum_one.tile([P, WARM_COLS], F32, tag="bank")
+            nc.tensor.matmul(out=unread[:], lhsT=zeros[:, 0:P], rhs=zeros[:], start=True, stop=True)
 
         x_grouped = keep.tile([P, WINDOWS * TOK * PACK], BF16, align_bytes=64)
         nc.vector.memset(x_grouped[:], 0.0)

@@ -34,6 +34,7 @@ VECTOR_COLS = 160
 
 WARM_COLS = 256
 WARM_PASSES = 2
+HL_WAIT_PASSES = 4
 
 FLOPS = 2 * TOK * (WINDOWS * NIN) * H + 2 * TOK * H * (NOUT * H)
 
@@ -42,8 +43,8 @@ def tile_bilinearpairedlayer_pa_s_kernel(tc, x_l, W_l, b_l, W_bil, out):
     nc = tc.nc
     with ExitStack() as ctx:
         keep = ctx.enter_context(tc.tile_pool(name="keep", bufs=1))
-        psum_one = ctx.enter_context(tc.psum_pool(name="psum_one", bufs=6))
-        psum_two = ctx.enter_context(tc.psum_pool(name="psum_two", bufs=2))
+        psum_one = ctx.enter_context(tc.psum_pool(name="psum_one", bufs=4))
+        psum_two = ctx.enter_context(tc.psum_pool(name="psum_two", bufs=4))
         ctx.enter_context(tc.manual_schedule())
 
         x_raw = keep.tile([P, NIN], BF16)
@@ -174,7 +175,7 @@ def tile_bilinearpairedlayer_pa_s_kernel(tc, x_l, W_l, b_l, W_bil, out):
         out_rows = out.rearrange("b i k g -> (b i) (k g)")
 
         def layer2_unit(q):
-            acc = psum_two.tile([P, UNIT], F32)
+            acc = psum_two.tile([P, UNIT], F32, tag="acc")
             nc.tensor.matmul_mx(
                 out=acc[:],
                 lhsT=hl_codes[:].bitcast(FP8X4),
@@ -191,6 +192,19 @@ def tile_bilinearpairedlayer_pa_s_kernel(tc, x_l, W_l, b_l, W_bil, out):
                 nc.vector.tensor_copy(out=result[:], in_=acc[:])
             nc.sync.dma_start(out=out_rows[:, q * UNIT : (q + 1) * UNIT], in_=result[:])
 
+        def stay_warm():
+            for i in range(HL_WAIT_PASSES):
+                unread = psum_two.tile([P, UNIT], F32, tag="acc")
+                nc.tensor.matmul_mx(
+                    out=unread[:],
+                    lhsT=x_codes[:, 0, :].bitcast(FP8X4),
+                    lhsT_scale=x_scales[:, 0, :],
+                    rhs=wb_codes[:, 0, :].bitcast(FP8X4),
+                    rhs_scale=wb_scales[:, 0, :],
+                    start=True,
+                    stop=True,
+                )
+
         regroup_unit(0)
         for t in range(H_TILES):
             relu_tile(t, layer1_tile(t))
@@ -200,6 +214,7 @@ def tile_bilinearpairedlayer_pa_s_kernel(tc, x_l, W_l, b_l, W_bil, out):
         regroup_hl()
         quantise_unit(1)
         quantise_hl()
+        stay_warm()
         regroup_unit(3)
         quantise_unit(2)
         quantise_unit(3)

@@ -27,9 +27,8 @@ ITEMS_PER_BANK = 2
 WL_BANKS = ITEMS // ITEMS_PER_BANK
 WL_CHUNK = ITEMS_PER_BANK * NIN
 
-UNIT = 256
-UNITS = NOUT * H // UNIT
-UNITS_PER_MAP = H // UNIT
+UNITS = ((0, 256), (256, 256), (512, 256), (768, 128), (896, 128))
+WIDE = 256
 VECTOR_COLS = 160
 
 WARM_COLS = 256
@@ -94,29 +93,75 @@ def tile_bilinearpairedlayer_pa_s_kernel(tc, x_l, W_l, b_l, W_bil, out):
                 in_=x_grouped[:, c * TOK * PACK : (c + 1) * TOK * PACK],
             )
 
+        wb_grouped = keep.tile([P, NOUT * H, PACK], BF16, align_bytes=64)
+        wb_codes = keep.tile([P, NOUT * H], U32, align_bytes=64)
+        wb_scales = keep.tile([P, NOUT * H], U8, align_bytes=64)
+
+        def regroup_wb(copy, first, last):
+            raw = wb_raw[first // H]
+            g0 = first // H * H
+            copy(
+                out=wb_grouped[:, first:last, :].rearrange("p (c i) t -> p c t i", i=4),
+                in_=raw[:, :, first - g0 : last - g0].rearrange("p t (c i) -> p c t i", i=4),
+            )
+
+        def regroup_unit(q):
+            first, width = UNITS[q]
+            if width == WIDE:
+                regroup_wb(nc.vector.tensor_copy, first, first + VECTOR_COLS)
+                regroup_wb(nc.scalar.copy, first + VECTOR_COLS, first + width)
+            else:
+                regroup_wb(nc.scalar.copy, first, first + width)
+
+        def quantise_unit(q):
+            first, width = UNITS[q]
+            nc.vector.quantize_mx(
+                out=wb_codes[:, first : first + width].bitcast(FP8X4),
+                scales=wb_scales[:, first : first + width],
+                in_=wb_grouped[:, first : first + width, :].rearrange("p g t -> p (g t)"),
+            )
+
         wl_grouped = keep.tile([P, ITEMS * P * PACK], BF16, align_bytes=64)
         wlg_words = wl_grouped[:].bitcast(F32).rearrange("p (a h u) -> p a h u", a=ITEMS, u=HALVES)
         wl_codes = keep.tile([P, ITEMS * P], U32, align_bytes=64)
         wl_scales = keep.tile([P, ITEMS * P], U8, align_bytes=64)
-        for n in range(WL_BANKS):
-            wl_words = wl_raw[n][:].bitcast(F32)
-            wT = psum_one.tile([P, ITEMS_PER_BANK * HALVES, P], F32, tag="bank")
-            for j in range(ITEMS_PER_BANK * HALVES):
-                nc.tensor.transpose(wT[:, j, :], wl_words[:, (j // HALVES) * HALVES * P + j % HALVES : (j // HALVES + 1) * HALVES * P : HALVES], ident[:])
-            nc.scalar.copy(
-                out=wlg_words[:, n * ITEMS_PER_BANK : (n + 1) * ITEMS_PER_BANK, :, :],
+
+        def regroup_wl(copy, first, count):
+            wl_words = wl_raw[first // ITEMS_PER_BANK][:].bitcast(F32)
+            wT = psum_one.tile([P, count * HALVES, P], F32, tag="bank")
+            for a in range(count):
+                w0 = ((first + a) % ITEMS_PER_BANK) * HALVES * P
+                for u in range(HALVES):
+                    nc.tensor.transpose(
+                        wT[:, a * HALVES + u, :], wl_words[:, w0 + u : w0 + HALVES * P : HALVES], ident[:]
+                    )
+            copy(
+                out=wlg_words[:, first : first + count, :, :],
                 in_=wT[:].rearrange("p (a u) h -> p a h u", u=HALVES),
             )
+
+        def quantise_wl(first, count):
             nc.vector.quantize_mx(
-                out=wl_codes[:, n * ITEMS_PER_BANK * P : (n + 1) * ITEMS_PER_BANK * P].bitcast(FP8X4),
-                scales=wl_scales[:, n * ITEMS_PER_BANK * P : (n + 1) * ITEMS_PER_BANK * P],
-                in_=wl_grouped[:, n * WL_CHUNK : (n + 1) * WL_CHUNK],
+                out=wl_codes[:, first * P : (first + count) * P].bitcast(FP8X4),
+                scales=wl_scales[:, first * P : (first + count) * P],
+                in_=wl_grouped[:, first * P * PACK : (first + count) * P * PACK],
             )
+
+        for n in range(WL_BANKS - 1):
+            regroup_wl(nc.scalar.copy, n * ITEMS_PER_BANK, ITEMS_PER_BANK)
+            if n < WL_BANKS - 2:
+                quantise_wl(n * ITEMS_PER_BANK, ITEMS_PER_BANK)
+        regroup_wl(nc.scalar.copy, ITEMS - 2, 1)
+        regroup_wl(nc.vector.tensor_copy, ITEMS - 1, 1)
+        quantise_wl(ITEMS - 4, 2)
+        regroup_unit(0)
+        quantise_wl(ITEMS - 2, 1)
+        quantise_wl(ITEMS - 1, 1)
 
         hlT = keep.tile([P, H_TILES, TOK], BF16)
 
         def layer1_tile(t):
-            pre = psum_one.tile([P, TOK], F32, tag="bank")
+            pre = psum_one.tile([P, TOK], F32, tag="bank", name="pre%d" % t)
             for c in range(WINDOWS):
                 a = t * WINDOWS + c
                 nc.tensor.matmul_mx(
@@ -135,29 +180,6 @@ def tile_bilinearpairedlayer_pa_s_kernel(tc, x_l, W_l, b_l, W_bil, out):
                 out=hlT[:, t, :], in_=pre[:], func=RELU, bias=bias[:, t : t + 1], scale=1.0
             )
 
-        wb_grouped = keep.tile([P, UNITS, UNIT, PACK], BF16, align_bytes=64)
-        wb_codes = keep.tile([P, UNITS, UNIT], U32, align_bytes=64)
-        wb_scales = keep.tile([P, UNITS, UNIT], U8, align_bytes=64)
-
-        def regroup_unit(q):
-            raw = wb_raw[q // UNITS_PER_MAP]
-            g0 = (q % UNITS_PER_MAP) * UNIT
-            nc.vector.tensor_copy(
-                out=wb_grouped[:, q, 0:VECTOR_COLS, :].rearrange("p (c i) t -> p c t i", i=4),
-                in_=raw[:, :, g0 : g0 + VECTOR_COLS].rearrange("p t (c i) -> p c t i", i=4),
-            )
-            nc.scalar.copy(
-                out=wb_grouped[:, q, VECTOR_COLS:UNIT, :].rearrange("p (c i) t -> p c t i", i=4),
-                in_=raw[:, :, g0 + VECTOR_COLS : g0 + UNIT].rearrange("p t (c i) -> p c t i", i=4),
-            )
-
-        def quantise_unit(q):
-            nc.vector.quantize_mx(
-                out=wb_codes[:, q, :].bitcast(FP8X4),
-                scales=wb_scales[:, q, :],
-                in_=wb_grouped[:, q, :, :].rearrange("p g t -> p (g t)"),
-            )
-
         hl_grouped = keep.tile([P, TOK, PACK], BF16, align_bytes=64)
         hl_codes = keep.tile([P, TOK], U32, align_bytes=64)
         hl_scales = keep.tile([P, TOK], U8, align_bytes=64)
@@ -174,49 +196,57 @@ def tile_bilinearpairedlayer_pa_s_kernel(tc, x_l, W_l, b_l, W_bil, out):
 
         out_rows = out.rearrange("b i k g -> (b i) (k g)")
 
-        def layer2_unit(q):
-            acc = psum_two.tile([P, UNIT], F32, tag="acc")
+        def layer2_unit(q, copy):
+            first, width = UNITS[q]
+            if width == WIDE:
+                acc = psum_two.tile([P, WIDE], F32, tag="acc")
+            else:
+                acc = psum_one.tile([P, WIDE], F32, tag="bank")
             nc.tensor.matmul_mx(
-                out=acc[:],
+                out=acc[:, 0:width],
                 lhsT=hl_codes[:].bitcast(FP8X4),
                 lhsT_scale=hl_scales[:],
-                rhs=wb_codes[:, q, :].bitcast(FP8X4),
-                rhs_scale=wb_scales[:, q, :],
+                rhs=wb_codes[:, first : first + width].bitcast(FP8X4),
+                rhs_scale=wb_scales[:, first : first + width],
                 start=True,
                 stop=True,
             )
-            result = keep.tile([P, UNIT], F32, name="result%d" % q)
-            if q % 2 == 0:
-                nc.scalar.copy(out=result[:], in_=acc[:])
-            else:
-                nc.vector.tensor_copy(out=result[:], in_=acc[:])
-            nc.sync.dma_start(out=out_rows[:, q * UNIT : (q + 1) * UNIT], in_=result[:])
+            result = keep.tile([P, width], F32, name="result%d" % q)
+            copy(out=result[:], in_=acc[:, 0:width])
+            nc.sync.dma_start(out=out_rows[:, first : first + width], in_=result[:])
 
         def stay_warm():
             for i in range(HL_WAIT_PASSES):
-                unread = psum_two.tile([P, UNIT], F32, tag="acc")
+                unread = psum_two.tile([P, WIDE], F32, tag="acc")
                 nc.tensor.matmul_mx(
                     out=unread[:],
                     lhsT=x_codes[:, 0, :].bitcast(FP8X4),
                     lhsT_scale=x_scales[:, 0, :],
-                    rhs=wb_codes[:, 0, :].bitcast(FP8X4),
-                    rhs_scale=wb_scales[:, 0, :],
+                    rhs=wl_codes[:, 0:WIDE].bitcast(FP8X4),
+                    rhs_scale=wl_scales[:, 0:WIDE],
                     start=True,
                     stop=True,
                 )
 
-        regroup_unit(0)
-        for t in range(H_TILES):
-            relu_tile(t, layer1_tile(t))
+        pre = [layer1_tile(t) for t in range(H_TILES)]
+        stay_warm()
+        relu_tile(0, pre[0])
+        relu_tile(1, pre[1])
         regroup_unit(1)
-        regroup_unit(2)
+        relu_tile(2, pre[2])
+        relu_tile(3, pre[3])
         quantise_unit(0)
         regroup_hl()
-        quantise_unit(1)
+        regroup_unit(2)
         quantise_hl()
-        stay_warm()
         regroup_unit(3)
+        regroup_unit(4)
+        quantise_unit(1)
+        layer2_unit(0, nc.scalar.copy)
         quantise_unit(2)
+        layer2_unit(1, nc.scalar.copy)
         quantise_unit(3)
-        for q in range(UNITS):
-            layer2_unit(q)
+        quantise_unit(4)
+        layer2_unit(2, nc.vector.tensor_copy)
+        layer2_unit(3, nc.scalar.copy)
+        layer2_unit(4, nc.vector.tensor_copy)

@@ -23,13 +23,13 @@ NOUT = 2
 
 HALVES = 2
 ITEMS = H_TILES * WINDOWS
-ITEMS_PER_BANK = 2
-WL_BANKS = ITEMS // ITEMS_PER_BANK
-WL_CHUNK = ITEMS_PER_BANK * NIN
+WL_GROUPS = ((0, 2), (2, 2), (4, 2), (6, 2), (8, 2), (10, 1), (11, 1))
 
 UNITS = ((0, 256), (256, 256), (512, 256), (768, 128), (896, 128))
 WIDE = 256
 VECTOR_COLS = 160
+
+ON_TENSOR = 4
 
 WARM_COLS = 256
 WARM_PASSES = 2
@@ -48,14 +48,14 @@ def tile_bilinearpairedlayer_pa_s_kernel(tc, x_l, W_l, b_l, W_bil, out):
 
         x_raw = keep.tile([P, NIN], BF16)
         nc.sync.dma_start(out=x_raw[:], in_=x_l.rearrange("b i f -> (b i) f"))
-        bias = keep.tile([P, PACK], BF16)
-        nc.scalar.dma_start(out=bias[:], in_=b_l.rearrange("(p t) -> p t", t=PACK))
         wl_rows = W_l.rearrange("(p t) f -> p (t f)", t=PACK)
-        wl_raw = []
-        for n in range(WL_BANKS):
-            chunk = keep.tile([P, WL_CHUNK], BF16, name="wl_raw%d" % n)
-            nc.sync.dma_start(out=chunk[:], in_=wl_rows[:, n * WL_CHUNK : (n + 1) * WL_CHUNK])
-            wl_raw.append(chunk)
+        wl_raw = {}
+        for first, count in WL_GROUPS:
+            chunk = keep.tile([P, count * NIN], BF16, name="wl_raw%d" % first)
+            nc.sync.dma_start(out=chunk[:], in_=wl_rows[:, first * NIN : (first + count) * NIN])
+            wl_raw[first] = chunk
+        bias = keep.tile([P, PACK], BF16)
+        nc.sync.dma_start(out=bias[:], in_=b_l.rearrange("(p t) -> p t", t=PACK))
         wb_raw = []
         for k in range(NOUT):
             chunk = keep.tile([P, PACK, H], BF16, name="wb_raw%d" % k)
@@ -105,9 +105,27 @@ def tile_bilinearpairedlayer_pa_s_kernel(tc, x_l, W_l, b_l, W_bil, out):
                 in_=raw[:, :, first - g0 : last - g0].rearrange("p t (c i) -> p c t i", i=4),
             )
 
+        ident_bf16 = keep.tile([P, P], BF16)
+        make_identity(nc, ident_bf16[:])
+
+        def regroup_on_tensor(first, last):
+            raw = wb_raw[first // H]
+            g0 = first // H * H
+            moved = psum_two.tile([P, last - first, PACK], BF16, tag="acc")
+            nc.tensor.matmul(
+                out=moved[:].rearrange("p g t -> p (g t)"),
+                lhsT=ident_bf16[:],
+                rhs=raw[:, :, first - g0 : last - g0].rearrange("p t g -> p g t"),
+                start=True,
+                stop=True,
+            )
+            nc.scalar.copy(out=wb_grouped[:, first:last, :], in_=moved[:])
+
         def regroup_unit(q):
             first, width = UNITS[q]
-            if width == WIDE:
+            if q == ON_TENSOR:
+                regroup_on_tensor(first, first + width)
+            elif width == WIDE:
                 regroup_wb(nc.vector.tensor_copy, first, first + VECTOR_COLS)
                 regroup_wb(nc.scalar.copy, first + VECTOR_COLS, first + width)
             else:
@@ -127,10 +145,10 @@ def tile_bilinearpairedlayer_pa_s_kernel(tc, x_l, W_l, b_l, W_bil, out):
         wl_scales = keep.tile([P, ITEMS * P], U8, align_bytes=64)
 
         def regroup_wl(copy, first, count):
-            wl_words = wl_raw[first // ITEMS_PER_BANK][:].bitcast(F32)
+            wl_words = wl_raw[first][:].bitcast(F32)
             wT = psum_one.tile([P, count * HALVES, P], F32, tag="bank")
             for a in range(count):
-                w0 = ((first + a) % ITEMS_PER_BANK) * HALVES * P
+                w0 = a * HALVES * P
                 for u in range(HALVES):
                     nc.tensor.transpose(
                         wT[:, a * HALVES + u, :], wl_words[:, w0 + u : w0 + HALVES * P : HALVES], ident[:]
@@ -147,16 +165,16 @@ def tile_bilinearpairedlayer_pa_s_kernel(tc, x_l, W_l, b_l, W_bil, out):
                 in_=wl_grouped[:, first * P * PACK : (first + count) * P * PACK],
             )
 
-        for n in range(WL_BANKS - 1):
-            regroup_wl(nc.scalar.copy, n * ITEMS_PER_BANK, ITEMS_PER_BANK)
-            if n < WL_BANKS - 2:
-                quantise_wl(n * ITEMS_PER_BANK, ITEMS_PER_BANK)
-        regroup_wl(nc.scalar.copy, ITEMS - 2, 1)
-        regroup_wl(nc.vector.tensor_copy, ITEMS - 1, 1)
-        quantise_wl(ITEMS - 4, 2)
+        for first, count in WL_GROUPS[:-3]:
+            regroup_wl(nc.scalar.copy, first, count)
+            quantise_wl(first, count)
+        regroup_wl(nc.scalar.copy, *WL_GROUPS[-3])
+        regroup_wl(nc.scalar.copy, *WL_GROUPS[-2])
+        regroup_wl(nc.vector.tensor_copy, *WL_GROUPS[-1])
+        quantise_wl(*WL_GROUPS[-3])
         regroup_unit(0)
-        quantise_wl(ITEMS - 2, 1)
-        quantise_wl(ITEMS - 1, 1)
+        quantise_wl(*WL_GROUPS[-1])
+        quantise_wl(*WL_GROUPS[-2])
 
         hlT = keep.tile([P, H_TILES, TOK], BF16)
 

@@ -27,12 +27,8 @@ WL_GROUPS = ((0, 2), (2, 2), (4, 2), (6, 2), (8, 2), (10, 1), (11, 1))
 
 UNITS = ((0, 256), (256, 256), (512, 256), (768, 128), (896, 128))
 WIDE = 256
-VECTOR_COLS = 160
+VECTOR_COLS = 144
 
-ON_TENSOR = 4
-
-WARM_COLS = 256
-WARM_PASSES = 2
 HL_WAIT_PASSES = 4
 
 FLOPS = 2 * TOK * (WINDOWS * NIN) * H + 2 * TOK * H * (NOUT * H)
@@ -64,12 +60,6 @@ def tile_bilinearpairedlayer_pa_s_kernel(tc, x_l, W_l, b_l, W_bil, out):
 
         ident = keep.tile([P, P], F32)
         make_identity(nc, ident[:])
-
-        zeros = keep.tile([P, WARM_COLS], F32)
-        nc.vector.memset(zeros[:], 0.0)
-        for i in range(WARM_PASSES):
-            unread = psum_one.tile([P, WARM_COLS], F32, tag="bank")
-            nc.tensor.matmul(out=unread[:], lhsT=zeros[:, 0:P], rhs=zeros[:], start=True, stop=True)
 
         x_grouped = keep.tile([P, WINDOWS * TOK * PACK], BF16, align_bytes=64)
         nc.vector.memset(x_grouped[:], 0.0)
@@ -123,13 +113,11 @@ def tile_bilinearpairedlayer_pa_s_kernel(tc, x_l, W_l, b_l, W_bil, out):
 
         def regroup_unit(q):
             first, width = UNITS[q]
-            if q == ON_TENSOR:
-                regroup_on_tensor(first, first + width)
-            elif width == WIDE:
+            if width == WIDE:
                 regroup_wb(nc.vector.tensor_copy, first, first + VECTOR_COLS)
                 regroup_wb(nc.scalar.copy, first + VECTOR_COLS, first + width)
             else:
-                regroup_wb(nc.scalar.copy, first, first + width)
+                regroup_on_tensor(first, first + width)
 
         def quantise_unit(q):
             first, width = UNITS[q]

@@ -157,12 +157,10 @@ def tile_bilinearpairedlayer_pa_s_kernel(tc, x_l, W_l, b_l, W_bil, out):
             regroup_wl(nc.scalar.copy, first, count)
             quantise_wl(first, count)
         regroup_wl(nc.scalar.copy, *WL_GROUPS[-3])
-        regroup_wl(nc.scalar.copy, *WL_GROUPS[-2])
-        regroup_wl(nc.vector.tensor_copy, *WL_GROUPS[-1])
-        quantise_wl(*WL_GROUPS[-3])
-        regroup_unit(0)
-        quantise_wl(*WL_GROUPS[-1])
-        quantise_wl(*WL_GROUPS[-2])
+        regroup_wl(nc.vector.tensor_copy, *WL_GROUPS[-2])
+        regroup_wl(nc.scalar.copy, *WL_GROUPS[-1])
+        for first, count in WL_GROUPS[-3:]:
+            quantise_wl(first, count)
 
         hlT = keep.tile([P, H_TILES, TOK], BF16)
 
@@ -238,13 +236,14 @@ def tile_bilinearpairedlayer_pa_s_kernel(tc, x_l, W_l, b_l, W_bil, out):
         stay_warm()
         relu_tile(0, pre[0])
         relu_tile(1, pre[1])
-        regroup_unit(1)
+        regroup_unit(0)
         relu_tile(2, pre[2])
         relu_tile(3, pre[3])
-        quantise_unit(0)
+        regroup_unit(1)
         regroup_hl()
-        regroup_unit(2)
+        quantise_unit(0)
         quantise_hl()
+        regroup_unit(2)
         regroup_unit(3)
         regroup_unit(4)
         quantise_unit(1)

@@ -24,11 +24,17 @@ NOUT = 2
 HALVES = 2
 ITEMS = H_TILES * WINDOWS
 WL_GROUPS = ((0, 2), (2, 2), (4, 2), (6, 2), (8, 2), (10, 1), (11, 1))
+BIAS_BEFORE = 4
+BIAS_USED_BEFORE = 6
 
 UNITS = ((0, 256), (256, 256), (512, 256), (768, 128), (896, 128))
 WIDE = 256
-VECTOR_COLS = 144
+VECTOR_COLS = (144, 144, 208)
 
+ON_TENSOR = 4
+
+WARM_COLS = 256
+WARM_PASSES = 2
 HL_WAIT_PASSES = 4
 
 FLOPS = 2 * TOK * (WINDOWS * NIN) * H + 2 * TOK * H * (NOUT * H)
@@ -42,16 +48,21 @@ def tile_bilinearpairedlayer_pa_s_kernel(tc, x_l, W_l, b_l, W_bil, out):
         psum_two = ctx.enter_context(tc.psum_pool(name="psum_two", bufs=4))
         ctx.enter_context(tc.manual_schedule())
 
+        zeros = keep.tile([P, WARM_COLS], F32)
+        nc.vector.memset(zeros[:], 0.0)
+
         x_raw = keep.tile([P, NIN], BF16)
         nc.sync.dma_start(out=x_raw[:], in_=x_l.rearrange("b i f -> (b i) f"))
         wl_rows = W_l.rearrange("(p t) f -> p (t f)", t=PACK)
+        bias_rows = keep.tile([P, H], BF16)
+        nc.vector.memset(bias_rows[:], 0.0)
         wl_raw = {}
         for first, count in WL_GROUPS:
+            if first == BIAS_BEFORE:
+                nc.sync.dma_start(out=bias_rows[0:1, :], in_=b_l.rearrange("(q h) -> q h", q=1))
             chunk = keep.tile([P, count * NIN], BF16, name="wl_raw%d" % first)
             nc.sync.dma_start(out=chunk[:], in_=wl_rows[:, first * NIN : (first + count) * NIN])
             wl_raw[first] = chunk
-        bias = keep.tile([P, PACK], BF16)
-        nc.sync.dma_start(out=bias[:], in_=b_l.rearrange("(p t) -> p t", t=PACK))
         wb_raw = []
         for k in range(NOUT):
             chunk = keep.tile([P, PACK, H], BF16, name="wb_raw%d" % k)
@@ -61,8 +72,11 @@ def tile_bilinearpairedlayer_pa_s_kernel(tc, x_l, W_l, b_l, W_bil, out):
         ident = keep.tile([P, P], F32)
         make_identity(nc, ident[:])
 
+        for i in range(WARM_PASSES):
+            unread = psum_one.tile([P, WARM_COLS], F32, tag="bank")
+            nc.tensor.matmul(out=unread[:], lhsT=zeros[:, 0:P], rhs=zeros[:], start=True, stop=True)
+
         x_grouped = keep.tile([P, WINDOWS * TOK * PACK], BF16, align_bytes=64)
-        nc.vector.memset(x_grouped[:], 0.0)
         x_words = x_raw[:].bitcast(F32)
         xT = psum_one.tile([P, HALVES, TOK], F32, tag="bank")
         for u in range(HALVES):
@@ -71,6 +85,8 @@ def tile_bilinearpairedlayer_pa_s_kernel(tc, x_l, W_l, b_l, W_bil, out):
         xg_words = x_grouped[:].bitcast(F32).rearrange(
             "p (c b i u) -> p c b i u", c=WINDOWS, b=BATCH, u=HALVES
         )
+        nc.vector.memset(xg_words[:, 1, :, 0:1, :], 0.0)
+        nc.vector.memset(xg_words[:, 2, :, SEQ - 1 : SEQ, :], 0.0)
         nc.vector.tensor_copy(out=xg_words[:, 0], in_=xT_view)
         nc.vector.tensor_copy(out=xg_words[:, 1, :, 1:SEQ, :], in_=xT_view[:, :, 0 : SEQ - 1, :])
         nc.vector.tensor_copy(out=xg_words[:, 2, :, 0 : SEQ - 1, :], in_=xT_view[:, :, 1:SEQ, :])
@@ -113,11 +129,13 @@ def tile_bilinearpairedlayer_pa_s_kernel(tc, x_l, W_l, b_l, W_bil, out):
 
         def regroup_unit(q):
             first, width = UNITS[q]
-            if width == WIDE:
-                regroup_wb(nc.vector.tensor_copy, first, first + VECTOR_COLS)
-                regroup_wb(nc.scalar.copy, first + VECTOR_COLS, first + width)
-            else:
+            if q == ON_TENSOR:
                 regroup_on_tensor(first, first + width)
+            elif width == WIDE:
+                regroup_wb(nc.vector.tensor_copy, first, first + VECTOR_COLS[q])
+                regroup_wb(nc.scalar.copy, first + VECTOR_COLS[q], first + width)
+            else:
+                regroup_wb(nc.scalar.copy, first, first + width)
 
         def quantise_unit(q):
             first, width = UNITS[q]
@@ -153,7 +171,13 @@ def tile_bilinearpairedlayer_pa_s_kernel(tc, x_l, W_l, b_l, W_bil, out):
                 in_=wl_grouped[:, first * P * PACK : (first + count) * P * PACK],
             )
 
+        bias_words = keep.tile([P, HALVES], F32)
         for first, count in WL_GROUPS[:-3]:
+            if first == BIAS_USED_BEFORE:
+                bT = psum_one.tile([P, HALVES, P], F32, tag="bank")
+                for u in range(HALVES):
+                    nc.tensor.transpose(bT[:, u, :], bias_rows[:].bitcast(F32)[:, u : HALVES * P : HALVES], ident[:])
+                nc.scalar.copy(out=bias_words[:], in_=bT[:, :, 0])
             regroup_wl(nc.scalar.copy, first, count)
             quantise_wl(first, count)
         regroup_wl(nc.scalar.copy, *WL_GROUPS[-3])
@@ -181,7 +205,7 @@ def tile_bilinearpairedlayer_pa_s_kernel(tc, x_l, W_l, b_l, W_bil, out):
 
         def relu_tile(t, pre):
             nc.scalar.activation(
-                out=hlT[:, t, :], in_=pre[:], func=RELU, bias=bias[:, t : t + 1], scale=1.0
+                out=hlT[:, t, :], in_=pre[:], func=RELU, bias=bias_words[:].bitcast(BF16)[:, t : t + 1], scale=1.0
             )
 
         hl_grouped = keep.tile([P, TOK, PACK], BF16, align_bytes=64)
@@ -240,10 +264,10 @@ def tile_bilinearpairedlayer_pa_s_kernel(tc, x_l, W_l, b_l, W_bil, out):
         relu_tile(2, pre[2])
         relu_tile(3, pre[3])
         regroup_unit(1)
-        regroup_hl()
         quantise_unit(0)
-        quantise_hl()
+        regroup_hl()
         regroup_unit(2)
+        quantise_hl()
         regroup_unit(3)
         regroup_unit(4)
         quantise_unit(1)

@@ -24,8 +24,6 @@ NOUT = 2
 HALVES = 2
 ITEMS = H_TILES * WINDOWS
 WL_GROUPS = ((0, 2), (2, 2), (4, 2), (6, 2), (8, 2), (10, 1), (11, 1))
-BIAS_BEFORE = 4
-BIAS_USED_BEFORE = 6
 
 UNITS = ((0, 256), (256, 256), (512, 256), (768, 128), (896, 128))
 WIDE = 256
@@ -33,8 +31,7 @@ VECTOR_COLS = (144, 144, 208)
 
 ON_TENSOR = 4
 
-WARM_COLS = 256
-WARM_PASSES = 2
+WARM_COLS = (256, 128)
 HL_WAIT_PASSES = 4
 
 FLOPS = 2 * TOK * (WINDOWS * NIN) * H + 2 * TOK * H * (NOUT * H)
@@ -48,21 +45,19 @@ def tile_bilinearpairedlayer_pa_s_kernel(tc, x_l, W_l, b_l, W_bil, out):
         psum_two = ctx.enter_context(tc.psum_pool(name="psum_two", bufs=4))
         ctx.enter_context(tc.manual_schedule())
 
-        zeros = keep.tile([P, WARM_COLS], F32)
+        zeros = keep.tile([P, WARM_COLS[0]], F32)
         nc.vector.memset(zeros[:], 0.0)
 
         x_raw = keep.tile([P, NIN], BF16)
         nc.sync.dma_start(out=x_raw[:], in_=x_l.rearrange("b i f -> (b i) f"))
         wl_rows = W_l.rearrange("(p t) f -> p (t f)", t=PACK)
-        bias_rows = keep.tile([P, H], BF16)
-        nc.vector.memset(bias_rows[:], 0.0)
         wl_raw = {}
         for first, count in WL_GROUPS:
-            if first == BIAS_BEFORE:
-                nc.sync.dma_start(out=bias_rows[0:1, :], in_=b_l.rearrange("(q h) -> q h", q=1))
             chunk = keep.tile([P, count * NIN], BF16, name="wl_raw%d" % first)
             nc.sync.dma_start(out=chunk[:], in_=wl_rows[:, first * NIN : (first + count) * NIN])
             wl_raw[first] = chunk
+        bias = keep.tile([P, PACK], BF16)
+        nc.sync.dma_start(out=bias[:], in_=b_l.rearrange("(p t) -> p t", t=PACK))
         wb_raw = []
         for k in range(NOUT):
             chunk = keep.tile([P, PACK, H], BF16, name="wb_raw%d" % k)
@@ -72,9 +67,9 @@ def tile_bilinearpairedlayer_pa_s_kernel(tc, x_l, W_l, b_l, W_bil, out):
         ident = keep.tile([P, P], F32)
         make_identity(nc, ident[:])
 
-        for i in range(WARM_PASSES):
-            unread = psum_one.tile([P, WARM_COLS], F32, tag="bank")
-            nc.tensor.matmul(out=unread[:], lhsT=zeros[:, 0:P], rhs=zeros[:], start=True, stop=True)
+        for cols in WARM_COLS:
+            unread = psum_one.tile([P, cols], F32, tag="bank")
+            nc.tensor.matmul(out=unread[:], lhsT=zeros[:, 0:P], rhs=zeros[:, 0:cols], start=True, stop=True)
 
         x_grouped = keep.tile([P, WINDOWS * TOK * PACK], BF16, align_bytes=64)
         x_words = x_raw[:].bitcast(F32)
@@ -171,13 +166,7 @@ def tile_bilinearpairedlayer_pa_s_kernel(tc, x_l, W_l, b_l, W_bil, out):
                 in_=wl_grouped[:, first * P * PACK : (first + count) * P * PACK],
             )
 
-        bias_words = keep.tile([P, HALVES], F32)
         for first, count in WL_GROUPS[:-3]:
-            if first == BIAS_USED_BEFORE:
-                bT = psum_one.tile([P, HALVES, P], F32, tag="bank")
-                for u in range(HALVES):
-                    nc.tensor.transpose(bT[:, u, :], bias_rows[:].bitcast(F32)[:, u : HALVES * P : HALVES], ident[:])
-                nc.scalar.copy(out=bias_words[:], in_=bT[:, :, 0])
             regroup_wl(nc.scalar.copy, first, count)
             quantise_wl(first, count)
         regroup_wl(nc.scalar.copy, *WL_GROUPS[-3])
@@ -205,7 +194,7 @@ def tile_bilinearpairedlayer_pa_s_kernel(tc, x_l, W_l, b_l, W_bil, out):
 
         def relu_tile(t, pre):
             nc.scalar.activation(
-                out=hlT[:, t, :], in_=pre[:], func=RELU, bias=bias_words[:].bitcast(BF16)[:, t : t + 1], scale=1.0
+                out=hlT[:, t, :], in_=pre[:], func=RELU, bias=bias[:, t : t + 1], scale=1.0
             )
 
         hl_grouped = keep.tile([P, TOK, PACK], BF16, align_bytes=64)

from contextlib import ExitStack

import concourse.mybir as mybir
from concourse.masks import make_identity

F32 = mybir.dt.float32
BF16 = mybir.dt.bfloat16
U32 = mybir.dt.uint32
U8 = mybir.dt.uint8
FP8X4 = mybir.dt.float8_e4m3fn_x4
RELU = mybir.ActivationFunctionType.Relu

P = 128
PACK = 4
BATCH = 2
SEQ = 64
TOK = BATCH * SEQ
NIN = 512
WINDOWS = 3
H = 512
H_TILES = H // P
NOUT = 2

HALVES = 2
ITEMS = H_TILES * WINDOWS
WL_GROUPS = ((0, 2), (2, 2), (4, 2), (6, 2), (8, 2), (10, 1), (11, 1))

UNITS = ((0, 256), (256, 256), (512, 256), (768, 128), (896, 128))
WIDE = 256
VECTOR_COLS = (144, 144, 208)

ON_TENSOR = 4

WARM_COLS = (256, 128)
HL_WAIT_PASSES = 4

FLOPS = 2 * TOK * (WINDOWS * NIN) * H + 2 * TOK * H * (NOUT * H)


def tile_bilinearpairedlayer_pa_s_kernel(tc, x_l, W_l, b_l, W_bil, out):
    nc = tc.nc
    with ExitStack() as ctx:
        keep = ctx.enter_context(tc.tile_pool(name="keep", bufs=1))
        psum_one = ctx.enter_context(tc.psum_pool(name="psum_one", bufs=4))
        psum_two = ctx.enter_context(tc.psum_pool(name="psum_two", bufs=4))
        ctx.enter_context(tc.manual_schedule())

        zeros = keep.tile([P, WARM_COLS[0]], F32)
        nc.vector.memset(zeros[:], 0.0)

        x_raw = keep.tile([P, NIN], BF16)
        nc.sync.dma_start(out=x_raw[:], in_=x_l.rearrange("b i f -> (b i) f"))
        wl_rows = W_l.rearrange("(p t) f -> p (t f)", t=PACK)
        wl_raw = {}
        for first, count in WL_GROUPS:
            chunk = keep.tile([P, count * NIN], BF16, name="wl_raw%d" % first)
            nc.sync.dma_start(out=chunk[:], in_=wl_rows[:, first * NIN : (first + count) * NIN])
            wl_raw[first] = chunk
        bias = keep.tile([P, PACK], BF16)
        nc.sync.dma_start(out=bias[:], in_=b_l.rearrange("(p t) -> p t", t=PACK))
        wb_raw = []
        for k in range(NOUT):
            chunk = keep.tile([P, PACK, H], BF16, name="wb_raw%d" % k)
            nc.sync.dma_start(out=chunk[:], in_=W_bil[k].rearrange("(p t) g -> p t g", t=PACK))
            wb_raw.append(chunk)

        ident = keep.tile([P, P], F32)
        make_identity(nc, ident[:])

        for cols in WARM_COLS:
            unread = psum_one.tile([P, cols], F32, tag="bank")
            nc.tensor.matmul(out=unread[:], lhsT=zeros[:, 0:P], rhs=zeros[:, 0:cols], start=True, stop=True)

        x_grouped = keep.tile([P, WINDOWS * TOK * PACK], BF16, align_bytes=64)
        x_words = x_raw[:].bitcast(F32)
        xT = psum_one.tile([P, HALVES, TOK], F32, tag="bank")
        for u in range(HALVES):
            nc.tensor.transpose(xT[:, u, :], x_words[:, u : HALVES * P : HALVES], ident[:])
        xT_view = xT[:].rearrange("p u (b i) -> p b i u", b=BATCH)
        xg_words = x_grouped[:].bitcast(F32).rearrange(
            "p (c b i u) -> p c b i u", c=WINDOWS, b=BATCH, u=HALVES
        )
        nc.vector.memset(xg_words[:, 1, :, 0:1, :], 0.0)
        nc.vector.memset(xg_words[:, 2, :, SEQ - 1 : SEQ, :], 0.0)
        nc.vector.tensor_copy(out=xg_words[:, 0], in_=xT_view)
        nc.vector.tensor_copy(out=xg_words[:, 1, :, 1:SEQ, :], in_=xT_view[:, :, 0 : SEQ - 1, :])
        nc.vector.tensor_copy(out=xg_words[:, 2, :, 0 : SEQ - 1, :], in_=xT_view[:, :, 1:SEQ, :])
        x_codes = keep.tile([P, WINDOWS, TOK], U32, align_bytes=64)
        x_scales = keep.tile([P, WINDOWS, TOK], U8, align_bytes=64)
        for c in range(WINDOWS):
            nc.vector.quantize_mx(
                out=x_codes[:, c, :].bitcast(FP8X4),
                scales=x_scales[:, c, :],
                in_=x_grouped[:, c * TOK * PACK : (c + 1) * TOK * PACK],
            )

        wb_grouped = keep.tile([P, NOUT * H, PACK], BF16, align_bytes=64)
        wb_codes = keep.tile([P, NOUT * H], U32, align_bytes=64)
        wb_scales = keep.tile([P, NOUT * H], U8, align_bytes=64)

        def regroup_wb(copy, first, last):
            raw = wb_raw[first // H]
            g0 = first // H * H
            copy(
                out=wb_grouped[:, first:last, :].rearrange("p (c i) t -> p c t i", i=4),
                in_=raw[:, :, first - g0 : last - g0].rearrange("p t (c i) -> p c t i", i=4),
            )

        ident_bf16 = keep.tile([P, P], BF16)
        make_identity(nc, ident_bf16[:])

        def regroup_on_tensor(first, last):
            raw = wb_raw[first // H]
            g0 = first // H * H
            moved = psum_two.tile([P, last - first, PACK], BF16, tag="acc")
            nc.tensor.matmul(
                out=moved[:].rearrange("p g t -> p (g t)"),
                lhsT=ident_bf16[:],
                rhs=raw[:, :, first - g0 : last - g0].rearrange("p t g -> p g t"),
                start=True,
                stop=True,
            )
            nc.scalar.copy(out=wb_grouped[:, first:last, :], in_=moved[:])

        def regroup_unit(q):
            first, width = UNITS[q]
            if q == ON_TENSOR:
                regroup_on_tensor(first, first + width)
            elif width == WIDE:
                regroup_wb(nc.vector.tensor_copy, first, first + VECTOR_COLS[q])
                regroup_wb(nc.scalar.copy, first + VECTOR_COLS[q], first + width)
            else:
                regroup_wb(nc.scalar.copy, first, first + width)

        def quantise_unit(q):
            first, width = UNITS[q]
            nc.vector.quantize_mx(
                out=wb_codes[:, first : first + width].bitcast(FP8X4),
                scales=wb_scales[:, first : first + width],
                in_=wb_grouped[:, first : first + width, :].rearrange("p g t -> p (g t)"),
            )

        wl_grouped = keep.tile([P, ITEMS * P * PACK], BF16, align_bytes=64)
        wlg_words = wl_grouped[:].bitcast(F32).rearrange("p (a h u) -> p a h u", a=ITEMS, u=HALVES)
        wl_codes = keep.tile([P, ITEMS * P], U32, align_bytes=64)
        wl_scales = keep.tile([P, ITEMS * P], U8, align_bytes=64)

        def regroup_wl(copy, first, count):
            wl_words = wl_raw[first][:].bitcast(F32)
            wT = psum_one.tile([P, count * HALVES, P], F32, tag="bank")
            for a in range(count):
                w0 = a * HALVES * P
                for u in range(HALVES):
                    nc.tensor.transpose(
                        wT[:, a * HALVES + u, :], wl_words[:, w0 + u : w0 + HALVES * P : HALVES], ident[:]
                    )
            copy(
                out=wlg_words[:, first : first + count, :, :],
                in_=wT[:].rearrange("p (a u) h -> p a h u", u=HALVES),
            )

        def quantise_wl(first, count):
            nc.vector.quantize_mx(
                out=wl_codes[:, first * P : (first + count) * P].bitcast(FP8X4),
                scales=wl_scales[:, first * P : (first + count) * P],
                in_=wl_grouped[:, first * P * PACK : (first + count) * P * PACK],
            )

        for first, count in WL_GROUPS[:-3]:
            regroup_wl(nc.scalar.copy, first, count)
            quantise_wl(first, count)
        regroup_wl(nc.scalar.copy, *WL_GROUPS[-3])
        regroup_wl(nc.vector.tensor_copy, *WL_GROUPS[-2])
        regroup_wl(nc.scalar.copy, *WL_GROUPS[-1])
        for first, count in WL_GROUPS[-3:]:
            quantise_wl(first, count)

        hlT = keep.tile([P, H_TILES, TOK], BF16)

        def layer1_tile(t):
            pre = psum_one.tile([P, TOK], F32, tag="bank", name="pre%d" % t)
            for c in range(WINDOWS):
                a = t * WINDOWS + c
                nc.tensor.matmul_mx(
                    out=pre[:],
                    lhsT=wl_codes[:, a * P : (a + 1) * P].bitcast(FP8X4),
                    lhsT_scale=wl_scales[:, a * P : (a + 1) * P],
                    rhs=x_codes[:, c, :].bitcast(FP8X4),
                    rhs_scale=x_scales[:, c, :],
                    start=(c == 0),
                    stop=(c == WINDOWS - 1),
                )
            return pre

        def relu_tile(t, pre):
            nc.scalar.activation(
                out=hlT[:, t, :], in_=pre[:], func=RELU, bias=bias[:, t : t + 1], scale=1.0
            )

        hl_grouped = keep.tile([P, TOK, PACK], BF16, align_bytes=64)
        hl_codes = keep.tile([P, TOK], U32, align_bytes=64)
        hl_scales = keep.tile([P, TOK], U8, align_bytes=64)

        def regroup_hl():
            nc.vector.tensor_copy(out=hl_grouped[:], in_=hlT[:].rearrange("p t r -> p r t"))

        def quantise_hl():
            nc.vector.quantize_mx(
                out=hl_codes[:].bitcast(FP8X4),
                scales=hl_scales[:],
                in_=hl_grouped[:].rearrange("p r t -> p (r t)"),
            )

        out_rows = out.rearrange("b i k g -> (b i) (k g)")

        def layer2_unit(q, copy):
            first, width = UNITS[q]
            if width == WIDE:
                acc = psum_two.tile([P, WIDE], F32, tag="acc")
            else:
                acc = psum_one.tile([P, WIDE], F32, tag="bank")
            nc.tensor.matmul_mx(
                out=acc[:, 0:width],
                lhsT=hl_codes[:].bitcast(FP8X4),
                lhsT_scale=hl_scales[:],
                rhs=wb_codes[:, first : first + width].bitcast(FP8X4),
                rhs_scale=wb_scales[:, first : first + width],
                start=True,
                stop=True,
            )
            result = keep.tile([P, width], F32, name="result%d" % q)
            copy(out=result[:], in_=acc[:, 0:width])
            nc.sync.dma_start(out=out_rows[:, first : first + width], in_=result[:])

        def stay_warm():
            for i in range(HL_WAIT_PASSES):
                unread = psum_two.tile([P, WIDE], F32, tag="acc")
                nc.tensor.matmul_mx(
                    out=unread[:],
                    lhsT=x_codes[:, 0, :].bitcast(FP8X4),
                    lhsT_scale=x_scales[:, 0, :],
                    rhs=wl_codes[:, 0:WIDE].bitcast(FP8X4),
                    rhs_scale=wl_scales[:, 0:WIDE],
                    start=True,
                    stop=True,
                )

        pre = [layer1_tile(t) for t in range(H_TILES)]
        stay_warm()
        relu_tile(0, pre[0])
        relu_tile(1, pre[1])
        regroup_unit(0)
        relu_tile(2, pre[2])
        relu_tile(3, pre[3])
        regroup_unit(1)
        quantise_unit(0)
        regroup_hl()
        regroup_unit(2)
        quantise_hl()
        regroup_unit(3)
        regroup_unit(4)
        quantise_unit(1)
        layer2_unit(0, nc.scalar.copy)
        quantise_unit(2)
        layer2_unit(1, nc.scalar.copy)
        quantise_unit(3)
        quantise_unit(4)
        layer2_unit(2, nc.vector.tensor_copy)
        layer2_unit(3, nc.scalar.copy)
        layer2_unit(4, nc.vector.tensor_copy)
